import numpy as np
import ml_dtypes


def mxq(x, axis, fmt="e4m3"):
    dtype, down = {"e4m3": (ml_dtypes.float8_e4m3fn, 7), "e5m2": (ml_dtypes.float8_e5m2, 14)}[fmt]
    v = np.moveaxis(np.asarray(x, np.float32).astype(ml_dtypes.bfloat16).astype(np.float64), axis, -1)
    blocks = v.reshape(v.shape[:-1] + (-1, 32))
    amax = np.abs(blocks).max(-1, keepdims=True)
    byte = np.maximum(np.where(amax > 0, np.frexp(amax)[1] - 1 + 127, 0) - down, 1)
    scale = np.exp2(byte - 127.0)
    codes = (blocks / scale).astype(np.float32).astype(dtype).astype(np.float64)
    return np.moveaxis((codes * scale).reshape(v.shape), -1, axis)


WIDE = False


def mx_kscale(k):
    if not WIDE:
        return np.ones(k)
    levels = np.array([10, -10, 5, -5, 0])
    a = np.random.permutation(np.resize(levels, k // 512 * 4)).reshape(k // 512, 4)
    idx = np.arange(k)
    return np.exp2(a[idx // 512, idx % 128 // 32])


BF16 = ml_dtypes.bfloat16


def bf(x):
    return np.asarray(x, np.float32).astype(BF16)


def f64(x):
    return np.asarray(x).astype(np.float64)


B, S, D, N = 128, 32, 1024, 1024
EPS = 1e-5


def batch_bn(x, g, b):
    m = x.mean(axis=0)
    v = x.var(axis=0)
    return g * (x - m) / np.sqrt(v + EPS) + b


def setup_inputs():
    t, u = mx_kscale(D), mx_kscale(D)
    return {"s_z2": bf(np.random.standard_normal((B, S, D)) * 0.6 + np.random.standard_normal(D) * 0.4),
            "c_z2": bf(np.random.standard_normal((B, D)) * 0.6 + np.random.standard_normal(D) * 0.4),
            "s_g2": bf((1.0 + 0.1 * np.random.standard_normal(D)) * t),
            "s_be2": bf(0.1 * np.random.standard_normal(D) * t),
            "s_w3": bf(np.random.standard_normal((N, D)) * np.sqrt(2.0 / D) / t[None, :]),
            "s_b3": bf(0.1 * np.random.standard_normal(N)),
            "c_g2": bf((1.0 + 0.1 * np.random.standard_normal(D)) * u),
            "c_be2": bf(0.1 * np.random.standard_normal(D) * u),
            "c_w3": bf(np.random.standard_normal((N, D)) * np.sqrt(2.0 / D) / u[None, :]),
            "c_b3": bf(0.1 * np.random.standard_normal(N))}


def reference(s_z2, c_z2, s_g2, s_be2, s_w3, s_b3, c_g2, c_be2, c_w3, c_b3):
    c_h = np.maximum(batch_bn(f64(c_z2), f64(c_g2), f64(c_be2)), 0.0)
    c_out = (mxq(c_h, 1, "e4m3") @ mxq(f64(c_w3), 1, "e4m3").T) + f64(c_b3)
    s_h = np.maximum(batch_bn(f64(s_z2), f64(s_g2), f64(s_be2)), 0.0)
    s_p = (mxq(s_h, 2, "e4m3") @ mxq(f64(s_w3), 1, "e4m3").T) + f64(s_b3)
    s_out = s_p * c_out[:, None, :]
    aggregated_c = s_out.max(axis=1)
    return (s_out, aggregated_c)

@@ -1,0 +1,294 @@
+from contextlib import ExitStack
+
+import concourse.mybir as mybir
+from concourse.masks import make_identity
+
+F32 = mybir.dt.float32
+BF16 = mybir.dt.bfloat16
+U32 = mybir.dt.uint32
+U8 = mybir.dt.uint8
+FP8X4 = mybir.dt.float8_e4m3fn_x4
+ACT = mybir.ActivationFunctionType
+ALU = mybir.AluOpType
+
+P = 128
+SLICES = 32
+FEATURES = 1024
+OUTPUTS = 1024
+EPS = 1e-5
+PACK = 4
+PASSES = FEATURES // (P * PACK)
+QUARTERS = FEATURES // (2 * P)
+PER_PARTITION = FEATURES // P
+N_TILE = 512
+HALVES = OUTPUTS // N_TILE
+PAIR = 2
+CHUNK = 4
+
+FLOPS = 2 * (SLICES + 1) * P * FEATURES * OUTPUTS
+
+
+def tile_cgblock_pb_kernel(
+    tc, s_z2, c_z2, s_g2, s_be2, s_w3, s_b3, c_g2, c_be2, c_w3, c_b3, out_0, out_1
+):
+    nc = tc.nc
+    with ExitStack() as ctx:
+        consts = ctx.enter_context(tc.tile_pool(name="consts", bufs=1))
+        inputs = ctx.enter_context(tc.tile_pool(name="inputs", bufs=1))
+        weights = ctx.enter_context(tc.tile_pool(name="weights", bufs=1))
+        stage = ctx.enter_context(tc.tile_pool(name="stage", bufs=2))
+        stats = ctx.enter_context(tc.tile_pool(name="stats", bufs=3))
+        quantised = ctx.enter_context(tc.tile_pool(name="quantised", bufs=4))
+        results = ctx.enter_context(tc.tile_pool(name="results", bufs=3))
+        turned = ctx.enter_context(tc.psum_pool(name="turned", bufs=4))
+        sums = ctx.enter_context(tc.psum_pool(name="sums", bufs=1))
+        products = ctx.enter_context(tc.psum_pool(name="products", bufs=3))
+
+        identity = consts.tile([P, P], F32, name="identity")
+        make_identity(nc, identity[:])
+        minus_inv_batch = consts.tile([P, 1], BF16, name="minus_inv_batch")
+        nc.vector.memset(minus_inv_batch[:], -1.0 / P)
+        eps = consts.tile([P, 1], F32, name="eps")
+        nc.vector.memset(eps[:], EPS)
+        warm = consts.tile([P, 1], F32, name="warm")
+        nc.scalar.activation(out=warm[:], in_=eps[:], func=ACT.Sqrt)
+
+        vector_rows = consts.tile([P, P], F32, name="vector_rows")
+        nc.vector.memset(vector_rows[:], 0.0)
+        for v, vector in enumerate((s_g2, s_be2, c_g2, c_be2)):
+            nc.sync.dma_start(
+                out=vector_rows[:].bitcast(BF16)[QUARTERS * v : QUARTERS * (v + 1), :],
+                in_=vector.rearrange("(q w) -> q w", q=QUARTERS),
+            )
+
+        def load_slices(chunk):
+            rows = inputs.tile([P, CHUNK, FEATURES], BF16, name="s_rows%d" % chunk)
+            nc.sync.dma_start(out=rows[:], in_=s_z2[:, chunk * CHUNK : (chunk + 1) * CHUNK, :])
+            return rows
+
+        def load_weight(w, label):
+            halves = []
+            for half in range(HALVES):
+                rows = inputs.tile([P, N_TILE // P, FEATURES], BF16, name="%s%d" % (label, half))
+                nc.sync.dma_start(
+                    out=rows[:],
+                    in_=w[half * N_TILE : (half + 1) * N_TILE, :].rearrange("(c p) k -> p c k", p=P),
+                )
+                halves.append(rows)
+            return halves
+
+        def load_bias(b, label):
+            rows = consts.tile([P, OUTPUTS], BF16, name=label)
+            nc.sync.dma_start(out=rows[:], in_=b.partition_broadcast(P))
+            return rows
+
+        c_rows = inputs.tile([P, FEATURES], BF16, name="c_rows")
+        nc.sync.dma_start(out=c_rows[:], in_=c_z2)
+        s_rows = [load_slices(0)]
+        c_w_rows = load_weight(c_w3, "c_w_rows")
+        c_bias_rows = load_bias(c_b3, "c_bias_rows")
+        s_w_rows = load_weight(s_w3, "s_w_rows")
+        s_bias_rows = load_bias(s_b3, "s_bias_rows")
+        for chunk in range(1, SLICES // CHUNK):
+            s_rows.append(load_slices(chunk))
+
+        tables_ps = turned.tile([P, QUARTERS, P], F32, tag="turned", name="tables_ps")
+        nc.tensor.transpose(tables_ps[:, 0, :], vector_rows[:], identity[:])
+        tables = consts.tile([P, 4, PER_PARTITION], F32, name="tables")
+        nc.vector.tensor_copy(
+            out=tables[:].rearrange("p v j -> p (v j)"),
+            in_=tables_ps[:, 0, 0 : 4 * QUARTERS].bitcast(BF16),
+        )
+        s_gain, s_shift = tables[:, 0, :], tables[:, 1, :]
+        c_gain, c_shift = tables[:, 2, :], tables[:, 3, :]
+
+        def halves_of(xt):
+            return xt[:].bitcast(BF16).rearrange("p q (b e) -> p q e b", e=2)
+
+        def statistics(blocks, gain, shift):
+            shape = [P, len(blocks), PER_PARTITION]
+            mean_ps = sums.tile(shape, F32, tag="mean_ps", name="mean_ps")
+            neg_mean = stats.tile(shape, F32, tag="neg_mean", name="neg_mean")
+            sq_sum = stats.tile(shape, F32, tag="sq_sum", name="sq_sum")
+            turned_blocks = []
+            for s, rows in enumerate(blocks):
+                words = rows.bitcast(F32)
+                xt = turned.tile([P, QUARTERS, P], F32, tag="turned", name="xt")
+                for q in range(QUARTERS):
+                    nc.tensor.transpose(xt[:, q, :], words[:, q * P : (q + 1) * P], identity[:])
+                turned_blocks.append(xt)
+                by_parity = rows.rearrange("b (q p e) -> b q e p", q=QUARTERS, e=2)
+                for q in range(QUARTERS):
+                    for e in range(2):
+                        j = 2 * q + e
+                        nc.tensor.matmul(
+                            mean_ps[:, s, j : j + 1],
+                            lhsT=by_parity[:, q, e, :],
+                            rhs=minus_inv_batch[:],
+                            start=True,
+                            stop=True,
+                        )
+                nc.scalar.copy(out=neg_mean[:, s, :], in_=mean_ps[:, s, :])
+                squares = stage.tile([P, PER_PARTITION, P], BF16, tag="squares", name="squares")
+                for q in range(QUARTERS):
+                    for e in range(2):
+                        j = 2 * q + e
+                        nc.scalar.activation(
+                            out=squares[:, j, :],
+                            in_=halves_of(xt)[:, q, e, :],
+                            func=ACT.Square,
+                            bias=neg_mean[:, s, j : j + 1],
+                            scale=1.0,
+                            accum_out=sq_sum[:, s, j : j + 1],
+                        )
+            std = stats.tile(shape, F32, tag="std", name="std")
+            nc.scalar.activation(
+                out=std[:], in_=sq_sum[:], func=ACT.Sqrt, bias=eps[:], scale=1.0 / P
+            )
+            inv_std = stats.tile(shape, F32, tag="inv_std", name="inv_std")
+            nc.vector.reciprocal(out=inv_std[:], in_=std[:])
+            scale = stats.tile(shape, F32, tag="scale", name="scale")
+            nc.vector.tensor_tensor(
+                out=scale[:], in0=inv_std[:], in1=gain.unsqueeze(1).to_broadcast(shape), op=ALU.mult
+            )
+            centre = stats.tile(shape, F32, tag="centre", name="centre")
+            nc.vector.tensor_tensor(out=centre[:], in0=neg_mean[:], in1=scale[:], op=ALU.mult)
+            bias = stats.tile(shape, F32, tag="bias", name="bias")
+            nc.vector.tensor_tensor(
+                out=bias[:], in0=centre[:], in1=shift.unsqueeze(1).to_broadcast(shape), op=ALU.add
+            )
+            return turned_blocks, scale, bias
+
+        def activate_and_quantise(turned_blocks, scale, bias):
+            width = len(turned_blocks) * PASSES * P
+            hidden = stage.tile([P, PACK, width], BF16, tag="hidden", name="hidden")
+            for s, xt in enumerate(turned_blocks):
+                for q in range(QUARTERS):
+                    for e in range(2):
+                        j = 2 * q + e
+                        g, t = j // PACK, j % PACK
+                        first = (s * PASSES + g) * P
+                        nc.scalar.activation(
+                            out=hidden[:, t, first : first + P],
+                            in_=halves_of(xt)[:, q, e, :],
+                            func=ACT.Relu,
+                            bias=bias[:, s, j : j + 1],
+                            scale=scale[:, s, j : j + 1],
+                        )
+            grouped = stage.tile([P, width, PACK], BF16, tag="grouped", name="grouped", align_bytes=64)
+            nc.vector.tensor_copy(
+                out=grouped[:].rearrange("p (c i) t -> p c t i", i=4),
+                in_=hidden[:].rearrange("p t (c i) -> p c t i", i=4),
+            )
+            codes = quantised.tile([P, width], U32, tag="codes", name="codes", align_bytes=64)
+            planes = quantised.tile([P, width], U8, tag="planes", name="planes", align_bytes=64)
+            nc.vector.quantize_mx(
+                out=codes[:].bitcast(FP8X4),
+                scales=planes[:],
+                in_=grouped[:].rearrange("p w t -> p (w t)"),
+            )
+            return codes, planes
+
+        def quantise_weight(w_rows, label):
+            w_codes = weights.tile([P, PASSES, OUTPUTS], U32, name=label + "_codes", align_bytes=64)
+            w_planes = weights.tile([P, PASSES, OUTPUTS], U8, name=label + "_planes", align_bytes=64)
+            for half in range(HALVES):
+                words = w_rows[half][:].bitcast(F32)
+                cols = slice(half * N_TILE, (half + 1) * N_TILE)
+                for g in range(PASSES):
+                    grouped = stage.tile(
+                        [P, N_TILE, PACK], BF16, tag="w_grouped", name="w_grouped", align_bytes=64
+                    )
+                    grouped_words = grouped[:].bitcast(F32)
+                    for bank in range(2):
+                        wt = products.tile([P, 2, 2 * P], F32, tag="acc", name="wt")
+                        for u in range(2):
+                            q = 2 * g + u
+                            for c in range(2):
+                                nc.tensor.transpose(
+                                    wt[:, u, c * P : (c + 1) * P],
+                                    words[:, 2 * bank + c, q * P : (q + 1) * P],
+                                    identity[:],
+                                )
+                        target = grouped_words[:, bank * 2 * P : (bank + 1) * 2 * P, :]
+                        if bank == 0:
+                            nc.vector.tensor_copy(out=target, in_=wt[:].rearrange("p u n -> p n u"))
+                        else:
+                            nc.scalar.copy(out=target, in_=wt[:].rearrange("p u n -> p n u"))
+                    nc.vector.quantize_mx(
+                        out=w_codes[:, g, cols].bitcast(FP8X4),
+                        scales=w_planes[:, g, cols],
+                        in_=grouped[:].rearrange("p n t -> p (n t)"),
+                    )
+            return w_codes, w_planes
+
+        def project(codes, planes, s, w_codes, w_planes, half):
+            acc = products.tile([P, N_TILE], F32, tag="acc", name="acc")
+            cols = slice(half * N_TILE, (half + 1) * N_TILE)
+            for g in range(PASSES):
+                rows = slice((s * PASSES + g) * P, (s * PASSES + g + 1) * P)
+                nc.tensor.matmul_mx(
+                    out=acc[:],
+                    lhsT=codes[:, rows].bitcast(FP8X4),
+                    lhsT_scale=planes[:, rows],
+                    rhs=w_codes[:, g, cols].bitcast(FP8X4),
+                    rhs_scale=w_planes[:, g, cols],
+                    start=(g == 0),
+                    stop=(g == PASSES - 1),
+                )
+            return acc
+
+        c_codes, c_planes = activate_and_quantise(*statistics([c_rows[:]], c_gain, c_shift))
+        c_w_codes, c_w_planes = quantise_weight(c_w_rows, "c_w")
+        gate = consts.tile([P, OUTPUTS], F32, name="gate")
+        gated_bias = consts.tile([P, OUTPUTS], F32, name="gated_bias")
+        for half in range(HALVES):
+            cols = slice(half * N_TILE, (half + 1) * N_TILE)
+            acc = project(c_codes, c_planes, 0, c_w_codes, c_w_planes, half)
+            nc.vector.tensor_tensor(out=gate[:, cols], in0=acc[:], in1=c_bias_rows[:, cols], op=ALU.add)
+            nc.vector.tensor_tensor(
+                out=gated_bias[:, cols], in0=gate[:, cols], in1=s_bias_rows[:, cols], op=ALU.mult
+            )
+        s_w_codes, s_w_planes = quantise_weight(s_w_rows, "s_w")
+
+        best = consts.tile([P, PAIR, OUTPUTS], F32, name="best")
+
+        def gate_and_store(pair, codes, planes):
+            if pair == 0:
+                gated = best
+            else:
+                gated = results.tile([P, PAIR, OUTPUTS], F32, tag="gated", name="gated")
+            for s in range(PAIR):
+                for half in range(HALVES):
+                    cols = slice(half * N_TILE, (half + 1) * N_TILE)
+                    acc = project(codes, planes, s, s_w_codes, s_w_planes, half)
+                    nc.vector.tensor_tensor(
+                        out=gated[:, s, cols], in0=acc[:], in1=gate[:, cols], op=ALU.mult
+                    )
+                biased = results.tile([P, OUTPUTS], F32, tag="biased", name="biased")
+                nc.gpsimd.tensor_tensor(
+                    out=biased[:], in0=gated[:, s, :], in1=gated_bias[:], op=ALU.add
+                )
+                nc.sync.dma_start(out=out_0[:, pair * PAIR + s, :], in_=biased[:])
+            if pair > 0:
+                nc.vector.tensor_tensor(out=best[:], in0=best[:], in1=gated[:], op=ALU.max)
+
+        def blocks_of(pair):
+            first = pair * PAIR
+            return [s_rows[(first + s) // CHUNK][:, (first + s) % CHUNK, :] for s in range(PAIR)]
+
+        pairs = SLICES // PAIR
+        measured = {}
+        ready = {}
+        for step in range(pairs + 2):
+            if step < pairs:
+                measured[step] = statistics(blocks_of(step), s_gain, s_shift)
+            if 0 <= step - 1 < pairs:
+                ready[step - 1] = activate_and_quantise(*measured[step - 1])
+            if 0 <= step - 2:
+                gate_and_store(step - 2, *ready[step - 2])
+
+        pooled = results.tile([P, OUTPUTS], F32, tag="biased", name="pooled")
+        nc.vector.tensor_tensor(out=pooled[:], in0=best[:, 0, :], in1=best[:, 1, :], op=ALU.max)
+        nc.vector.tensor_tensor(out=pooled[:], in0=pooled[:], in1=gated_bias[:], op=ALU.add)
+        nc.sync.dma_start(out=out_1, in_=pooled[:])

@@ -266,7 +266,7 @@ def tile_cgblock_pb_kernel(
                         out=gated[:, s, cols], in0=acc[:], in1=gate[:, cols], op=ALU.mult
                     )
                 biased = results.tile([P, OUTPUTS], F32, tag="biased", name="biased")
-                nc.gpsimd.tensor_tensor(
+                nc.vector.tensor_tensor(
                     out=biased[:], in0=gated[:, s, :], in1=gated_bias[:], op=ALU.add
                 )
                 nc.sync.dma_start(out=out_0[:, pair * PAIR + s, :], in_=biased[:])

@@ -176,7 +176,7 @@ def tile_cgblock_pb_kernel(
                             scale=scale[:, s, j : j + 1],
                         )
             grouped = stage.tile([P, width, PACK], BF16, tag="grouped", name="grouped", align_bytes=64)
-            nc.vector.tensor_copy(
+            nc.scalar.copy(
                 out=grouped[:].rearrange("p (c i) t -> p c t i", i=4),
                 in_=hidden[:].rearrange("p t (c i) -> p c t i", i=4),
             )

@@ -23,6 +23,8 @@ PER_PARTITION = FEATURES // P
 N_TILE = 512
 HALVES = OUTPUTS // N_TILE
 PAIR = 2
+PAIRS = SLICES // PAIR
+CONTEXT = -1
 CHUNK = 4
 
 FLOPS = 2 * (SLICES + 1) * P * FEATURES * OUTPUTS
@@ -105,30 +107,48 @@ def tile_cgblock_pb_kernel(
         def halves_of(xt):
             return xt[:].bitcast(BF16).rearrange("p q (b e) -> p q e b", e=2)
 
-        def statistics(blocks, gain, shift):
-            shape = [P, len(blocks), PER_PARTITION]
-            mean_ps = sums.tile(shape, F32, tag="mean_ps", name="mean_ps")
-            neg_mean = stats.tile(shape, F32, tag="neg_mean", name="neg_mean")
+        def blocks_of(group):
+            if group == CONTEXT:
+                return [c_rows[:]]
+            first = group * PAIR
+            return [s_rows[(first + s) // CHUNK][:, (first + s) % CHUNK, :] for s in range(PAIR)]
+
+        def size_of(group):
+            return len(blocks_of(group)) if CONTEXT <= group < PAIRS else 0
+
+        xts, mean_ps, neg_mean, std = {}, {}, {}, {}
+        scale, bias, hidden, grouped, codes, planes = {}, {}, {}, {}, {}, {}
+
+        def turn(group, s):
+            rows = blocks_of(group)[s]
+            if s == 0:
+                xts[group] = []
+                mean_ps[group] = sums.tile(
+                    [P, size_of(group), PER_PARTITION], F32, tag="mean_ps", name="mean_ps"
+                )
+            words = rows.bitcast(F32)
+            xt = turned.tile([P, QUARTERS, P], F32, tag="turned", name="xt")
+            for q in range(QUARTERS):
+                nc.tensor.transpose(xt[:, q, :], words[:, q * P : (q + 1) * P], identity[:])
+            xts[group].append(xt)
+            by_parity = rows.rearrange("b (q p e) -> b q e p", q=QUARTERS, e=2)
+            for q in range(QUARTERS):
+                for e in range(2):
+                    j = 2 * q + e
+                    nc.tensor.matmul(
+                        mean_ps[group][:, s, j : j + 1],
+                        lhsT=by_parity[:, q, e, :],
+                        rhs=minus_inv_batch[:],
+                        start=True,
+                        stop=True,
+                    )
+
+        def spread(group):
+            shape = [P, size_of(group), PER_PARTITION]
+            neg_mean[group] = stats.tile(shape, F32, tag="neg_mean", name="neg_mean")
             sq_sum = stats.tile(shape, F32, tag="sq_sum", name="sq_sum")
-            turned_blocks = []
-            for s, rows in enumerate(blocks):
-                words = rows.bitcast(F32)
-                xt = turned.tile([P, QUARTERS, P], F32, tag="turned", name="xt")
-                for q in range(QUARTERS):
-                    nc.tensor.transpose(xt[:, q, :], words[:, q * P : (q + 1) * P], identity[:])
-                turned_blocks.append(xt)
-                by_parity = rows.rearrange("b (q p e) -> b q e p", q=QUARTERS, e=2)
-                for q in range(QUARTERS):
-                    for e in range(2):
-                        j = 2 * q + e
-                        nc.tensor.matmul(
-                            mean_ps[:, s, j : j + 1],
-                            lhsT=by_parity[:, q, e, :],
-                            rhs=minus_inv_batch[:],
-                            start=True,
-                            stop=True,
-                        )
-                nc.scalar.copy(out=neg_mean[:, s, :], in_=mean_ps[:, s, :])
+            for s, xt in enumerate(xts[group]):
+                nc.scalar.copy(out=neg_mean[group][:, s, :], in_=mean_ps[group][:, s, :])
                 squares = stage.tile([P, PER_PARTITION, P], BF16, tag="squares", name="squares")
                 for q in range(QUARTERS):
                     for e in range(2):
@@ -137,100 +157,129 @@ def tile_cgblock_pb_kernel(
                             out=squares[:, j, :],
                             in_=halves_of(xt)[:, q, e, :],
                             func=ACT.Square,
-                            bias=neg_mean[:, s, j : j + 1],
+                            bias=neg_mean[group][:, s, j : j + 1],
                             scale=1.0,
                             accum_out=sq_sum[:, s, j : j + 1],
                         )
-            std = stats.tile(shape, F32, tag="std", name="std")
+            std[group] = stats.tile(shape, F32, tag="std", name="std")
             nc.scalar.activation(
-                out=std[:], in_=sq_sum[:], func=ACT.Sqrt, bias=eps[:], scale=1.0 / P
+                out=std[group][:], in_=sq_sum[:], func=ACT.Sqrt, bias=eps[:], scale=1.0 / P
             )
+
+        def coefficient_steps(group):
+            shape = [P, size_of(group), PER_PARTITION]
+            gain, shift = (c_gain, c_shift) if group == CONTEXT else (s_gain, s_shift)
             inv_std = stats.tile(shape, F32, tag="inv_std", name="inv_std")
-            nc.vector.reciprocal(out=inv_std[:], in_=std[:])
-            scale = stats.tile(shape, F32, tag="scale", name="scale")
-            nc.vector.tensor_tensor(
-                out=scale[:], in0=inv_std[:], in1=gain.unsqueeze(1).to_broadcast(shape), op=ALU.mult
-            )
             centre = stats.tile(shape, F32, tag="centre", name="centre")
-            nc.vector.tensor_tensor(out=centre[:], in0=neg_mean[:], in1=scale[:], op=ALU.mult)
-            bias = stats.tile(shape, F32, tag="bias", name="bias")
-            nc.vector.tensor_tensor(
-                out=bias[:], in0=centre[:], in1=shift.unsqueeze(1).to_broadcast(shape), op=ALU.add
-            )
-            return turned_blocks, scale, bias
+            scale[group] = stats.tile(shape, F32, tag="scale", name="scale")
+            bias[group] = stats.tile(shape, F32, tag="bias", name="bias")
+            return [
+                lambda: nc.vector.reciprocal(out=inv_std[:], in_=std[group][:]),
+                lambda: nc.vector.tensor_tensor(
+                    out=scale[group][:],
+                    in0=inv_std[:],
+                    in1=gain.unsqueeze(1).to_broadcast(shape),
+                    op=ALU.mult,
+                ),
+                lambda: nc.vector.tensor_tensor(
+                    out=centre[:], in0=neg_mean[group][:], in1=scale[group][:], op=ALU.mult
+                ),
+                lambda: nc.vector.tensor_tensor(
+                    out=bias[group][:],
+                    in0=centre[:],
+                    in1=shift.unsqueeze(1).to_broadcast(shape),
+                    op=ALU.add,
+                ),
+            ]
 
-        def activate_and_quantise(turned_blocks, scale, bias):
-            width = len(turned_blocks) * PASSES * P
-            hidden = stage.tile([P, PACK, width], BF16, tag="hidden", name="hidden")
-            for s, xt in enumerate(turned_blocks):
-                for q in range(QUARTERS):
-                    for e in range(2):
-                        j = 2 * q + e
-                        g, t = j // PACK, j % PACK
-                        first = (s * PASSES + g) * P
-                        nc.scalar.activation(
-                            out=hidden[:, t, first : first + P],
-                            in_=halves_of(xt)[:, q, e, :],
-                            func=ACT.Relu,
-                            bias=bias[:, s, j : j + 1],
-                            scale=scale[:, s, j : j + 1],
-                        )
-            grouped = stage.tile([P, width, PACK], BF16, tag="grouped", name="grouped", align_bytes=64)
+        def activate(group, s):
+            if s == 0:
+                width = size_of(group) * PASSES * P
+                hidden[group] = stage.tile([P, PACK, width], BF16, tag="hidden", name="hidden")
+            for q in range(QUARTERS):
+                for e in range(2):
+                    j = 2 * q + e
+                    g, t = j // PACK, j % PACK
+                    first = (s * PASSES + g) * P
+                    nc.scalar.activation(
+                        out=hidden[group][:, t, first : first + P],
+                        in_=halves_of(xts[group][s])[:, q, e, :],
+                        func=ACT.Relu,
+                        bias=bias[group][:, s, j : j + 1],
+                        scale=scale[group][:, s, j : j + 1],
+                    )
+
+        def regroup_second_half(group):
+            width = size_of(group) * PASSES * P
+            middle = width // 2
+            grouped[group] = stage.tile(
+                [P, width, PACK], BF16, tag="grouped", name="grouped", align_bytes=64
+            )
             nc.scalar.copy(
-                out=grouped[:].rearrange("p (c i) t -> p c t i", i=4),
-                in_=hidden[:].rearrange("p t (c i) -> p c t i", i=4),
+                out=grouped[group][:, middle:, :].rearrange("p (c i) t -> p c t i", i=4),
+                in_=hidden[group][:, :, middle:].rearrange("p t (c i) -> p c t i", i=4),
             )
-            codes = quantised.tile([P, width], U32, tag="codes", name="codes", align_bytes=64)
-            planes = quantised.tile([P, width], U8, tag="planes", name="planes", align_bytes=64)
-            nc.vector.quantize_mx(
-                out=codes[:].bitcast(FP8X4),
-                scales=planes[:],
-                in_=grouped[:].rearrange("p w t -> p (w t)"),
-            )
-            return codes, planes
 
-        def quantise_weight(w_rows, label):
+        def regroup_first_half(group):
+            middle = size_of(group) * PASSES * P // 2
+            nc.vector.tensor_copy(
+                out=grouped[group][:, :middle, :].rearrange("p (c i) t -> p c t i", i=4),
+                in_=hidden[group][:, :, :middle].rearrange("p t (c i) -> p c t i", i=4),
+            )
+
+        def quantise(group):
+            width = size_of(group) * PASSES * P
+            codes[group] = quantised.tile([P, width], U32, tag="codes", name="codes", align_bytes=64)
+            planes[group] = quantised.tile([P, width], U8, tag="planes", name="planes", align_bytes=64)
+            nc.vector.quantize_mx(
+                out=codes[group][:].bitcast(FP8X4),
+                scales=planes[group][:],
+                in_=grouped[group][:].rearrange("p w t -> p (w t)"),
+            )
+
+        def weight_tiles(label):
             w_codes = weights.tile([P, PASSES, OUTPUTS], U32, name=label + "_codes", align_bytes=64)
             w_planes = weights.tile([P, PASSES, OUTPUTS], U8, name=label + "_planes", align_bytes=64)
-            for half in range(HALVES):
-                words = w_rows[half][:].bitcast(F32)
-                cols = slice(half * N_TILE, (half + 1) * N_TILE)
-                for g in range(PASSES):
-                    grouped = stage.tile(
-                        [P, N_TILE, PACK], BF16, tag="w_grouped", name="w_grouped", align_bytes=64
-                    )
-                    grouped_words = grouped[:].bitcast(F32)
-                    for bank in range(2):
-                        wt = products.tile([P, 2, 2 * P], F32, tag="acc", name="wt")
-                        for u in range(2):
-                            q = 2 * g + u
-                            for c in range(2):
-                                nc.tensor.transpose(
-                                    wt[:, u, c * P : (c + 1) * P],
-                                    words[:, 2 * bank + c, q * P : (q + 1) * P],
-                                    identity[:],
-                                )
-                        target = grouped_words[:, bank * 2 * P : (bank + 1) * 2 * P, :]
-                        if bank == 0:
-                            nc.vector.tensor_copy(out=target, in_=wt[:].rearrange("p u n -> p n u"))
-                        else:
-                            nc.scalar.copy(out=target, in_=wt[:].rearrange("p u n -> p n u"))
-                    nc.vector.quantize_mx(
-                        out=w_codes[:, g, cols].bitcast(FP8X4),
-                        scales=w_planes[:, g, cols],
-                        in_=grouped[:].rearrange("p n t -> p (n t)"),
-                    )
             return w_codes, w_planes
 
-        def project(codes, planes, s, w_codes, w_planes, half):
+        def quantise_weight_half(w_rows, w_codes, w_planes, half):
+            words = w_rows[half][:].bitcast(F32)
+            cols = slice(half * N_TILE, (half + 1) * N_TILE)
+            for g in range(PASSES):
+                grouped = stage.tile(
+                    [P, N_TILE, PACK], BF16, tag="w_grouped", name="w_grouped", align_bytes=64
+                )
+                grouped_words = grouped[:].bitcast(F32)
+                for bank in range(2):
+                    wt = products.tile([P, 2, 2 * P], F32, tag="acc", name="wt")
+                    for u in range(2):
+                        q = 2 * g + u
+                        for c in range(2):
+                            nc.tensor.transpose(
+                                wt[:, u, c * P : (c + 1) * P],
+                                words[:, 2 * bank + c, q * P : (q + 1) * P],
+                                identity[:],
+                            )
+                    target = grouped_words[:, bank * 2 * P : (bank + 1) * 2 * P, :]
+                    if bank == 0:
+                        nc.vector.tensor_copy(out=target, in_=wt[:].rearrange("p u n -> p n u"))
+                    else:
+                        nc.scalar.copy(out=target, in_=wt[:].rearrange("p u n -> p n u"))
+                nc.vector.quantize_mx(
+                    out=w_codes[:, g, cols].bitcast(FP8X4),
+                    scales=w_planes[:, g, cols],
+                    in_=grouped[:].rearrange("p n t -> p (n t)"),
+                )
+
+        def project(group, s, w_codes, w_planes, half):
             acc = products.tile([P, N_TILE], F32, tag="acc", name="acc")
             cols = slice(half * N_TILE, (half + 1) * N_TILE)
             for g in range(PASSES):
                 rows = slice((s * PASSES + g) * P, (s * PASSES + g + 1) * P)
                 nc.tensor.matmul_mx(
                     out=acc[:],
-                    lhsT=codes[:, rows].bitcast(FP8X4),
-                    lhsT_scale=planes[:, rows],
+                    lhsT=codes[group][:, rows].bitcast(FP8X4),
+                    lhsT_scale=planes[group][:, rows],
                     rhs=w_codes[:, g, cols].bitcast(FP8X4),
                     rhs_scale=w_planes[:, g, cols],
                     start=(g == 0),
@@ -238,55 +287,95 @@ def tile_cgblock_pb_kernel(
                 )
             return acc
 
-        c_codes, c_planes = activate_and_quantise(*statistics([c_rows[:]], c_gain, c_shift))
-        c_w_codes, c_w_planes = quantise_weight(c_w_rows, "c_w")
+        c_w_codes, c_w_planes = weight_tiles("c_w")
+        s_w_codes, s_w_planes = weight_tiles("s_w")
+
         gate = consts.tile([P, OUTPUTS], F32, name="gate")
         gated_bias = consts.tile([P, OUTPUTS], F32, name="gated_bias")
-        for half in range(HALVES):
-            cols = slice(half * N_TILE, (half + 1) * N_TILE)
-            acc = project(c_codes, c_planes, 0, c_w_codes, c_w_planes, half)
-            nc.vector.tensor_tensor(out=gate[:, cols], in0=acc[:], in1=c_bias_rows[:, cols], op=ALU.add)
-            nc.vector.tensor_tensor(
-                out=gated_bias[:, cols], in0=gate[:, cols], in1=s_bias_rows[:, cols], op=ALU.mult
-            )
-        s_w_codes, s_w_planes = quantise_weight(s_w_rows, "s_w")
-
         best = consts.tile([P, PAIR, OUTPUTS], F32, name="best")
+        gated = {}
 
-        def gate_and_store(pair, codes, planes):
+        def open_gate():
+            for half in range(HALVES):
+                cols = slice(half * N_TILE, (half + 1) * N_TILE)
+                acc = project(CONTEXT, 0, c_w_codes, c_w_planes, half)
+                nc.vector.tensor_tensor(
+                    out=gate[:, cols], in0=acc[:], in1=c_bias_rows[:, cols], op=ALU.add
+                )
+                nc.vector.tensor_tensor(
+                    out=gated_bias[:, cols], in0=gate[:, cols], in1=s_bias_rows[:, cols], op=ALU.mult
+                )
+
+        def multiply(pair):
             if pair == 0:
-                gated = best
+                gated[pair] = best
             else:
-                gated = results.tile([P, PAIR, OUTPUTS], F32, tag="gated", name="gated")
+                gated[pair] = results.tile([P, PAIR, OUTPUTS], F32, tag="gated", name="gated")
             for s in range(PAIR):
                 for half in range(HALVES):
                     cols = slice(half * N_TILE, (half + 1) * N_TILE)
-                    acc = project(codes, planes, s, s_w_codes, s_w_planes, half)
+                    acc = project(pair, s, s_w_codes, s_w_planes, half)
                     nc.vector.tensor_tensor(
-                        out=gated[:, s, cols], in0=acc[:], in1=gate[:, cols], op=ALU.mult
+                        out=gated[pair][:, s, cols], in0=acc[:], in1=gate[:, cols], op=ALU.mult
                     )
-                biased = results.tile([P, OUTPUTS], F32, tag="biased", name="biased")
-                nc.vector.tensor_tensor(
-                    out=biased[:], in0=gated[:, s, :], in1=gated_bias[:], op=ALU.add
-                )
-                nc.sync.dma_start(out=out_0[:, pair * PAIR + s, :], in_=biased[:])
+
+        def add_bias_and_store(pair, s):
+            biased = results.tile([P, OUTPUTS], F32, tag="biased", name="biased")
+            nc.vector.tensor_tensor(
+                out=biased[:], in0=gated[pair][:, s, :], in1=gated_bias[:], op=ALU.add
+            )
+            nc.sync.dma_start(out=out_0[:, pair * PAIR + s, :], in_=biased[:])
+
+        def pool(pair, s):
             if pair > 0:
-                nc.vector.tensor_tensor(out=best[:], in0=best[:], in1=gated[:], op=ALU.max)
+                nc.vector.tensor_tensor(
+                    out=best[:, s, :], in0=best[:, s, :], in1=gated[pair][:, s, :], op=ALU.max
+                )
 
-        def blocks_of(pair):
-            first = pair * PAIR
-            return [s_rows[(first + s) // CHUNK][:, (first + s) % CHUNK, :] for s in range(PAIR)]
+        def step(n):
+            if n == CONTEXT:
+                open_gate()
+            if n >= 0:
+                multiply(n)
+            if size_of(n + 2):
+                spread(n + 2)
+            for s in range(PAIR):
+                if s < size_of(n + 1):
+                    activate(n + 1, s)
+                if s < size_of(n + 3):
+                    turn(n + 3, s)
+            if size_of(n + 1):
+                regroup_second_half(n + 1)
+            long_steps = []
+            if n >= 0:
+                long_steps.append(lambda: add_bias_and_store(n, 0))
+            if size_of(n + 1):
+                long_steps.append(lambda: regroup_first_half(n + 1))
+            if n >= 0:
+                long_steps.append(lambda: add_bias_and_store(n, 1))
+            if size_of(n + 1):
+                long_steps.append(lambda: quantise(n + 1))
+            if n >= 0:
+                long_steps.append(lambda: pool(n, 0))
+                long_steps.append(lambda: pool(n, 1))
+            short_steps = coefficient_steps(n + 2) if size_of(n + 2) else []
+            for k in range(max(len(long_steps), len(short_steps))):
+                if k < len(long_steps):
+                    long_steps[k]()
+                if k < len(short_steps):
+                    short_steps[k]()
 
-        pairs = SLICES // PAIR
-        measured = {}
-        ready = {}
-        for step in range(pairs + 2):
-            if step < pairs:
-                measured[step] = statistics(blocks_of(step), s_gain, s_shift)
-            if 0 <= step - 1 < pairs:
-                ready[step - 1] = activate_and_quantise(*measured[step - 1])
-            if 0 <= step - 2:
-                gate_and_store(step - 2, *ready[step - 2])
+        step(CONTEXT - 3)
+        step(CONTEXT - 2)
+        for half in range(HALVES):
+            quantise_weight_half(c_w_rows, c_w_codes, c_w_planes, half)
+        step(CONTEXT - 1)
+        for half in range(HALVES):
+            quantise_weight_half(s_w_rows, s_w_codes, s_w_planes, half)
+        step(CONTEXT)
+        with tc.manual_schedule():
+            for n in range(PAIRS):
+                step(n)
 
         pooled = results.tile([P, OUTPUTS], F32, tag="biased", name="pooled")
         nc.vector.tensor_tensor(out=pooled[:], in0=best[:, 0, :], in1=best[:, 1, :], op=ALU.max)

from contextlib import ExitStack

import concourse.mybir as mybir
from concourse.masks import make_identity

F32 = mybir.dt.float32
BF16 = mybir.dt.bfloat16
U32 = mybir.dt.uint32
U8 = mybir.dt.uint8
FP8X4 = mybir.dt.float8_e4m3fn_x4
ACT = mybir.ActivationFunctionType
ALU = mybir.AluOpType

P = 128
SLICES = 32
FEATURES = 1024
OUTPUTS = 1024
EPS = 1e-5
PACK = 4
PASSES = FEATURES // (P * PACK)
QUARTERS = FEATURES // (2 * P)
PER_PARTITION = FEATURES // P
N_TILE = 512
HALVES = OUTPUTS // N_TILE
PAIR = 2
PAIRS = SLICES // PAIR
CONTEXT = -1
CHUNK = 4

FLOPS = 2 * (SLICES + 1) * P * FEATURES * OUTPUTS


def tile_cgblock_pb_kernel(
    tc, s_z2, c_z2, s_g2, s_be2, s_w3, s_b3, c_g2, c_be2, c_w3, c_b3, out_0, out_1
):
    nc = tc.nc
    with ExitStack() as ctx:
        consts = ctx.enter_context(tc.tile_pool(name="consts", bufs=1))
        inputs = ctx.enter_context(tc.tile_pool(name="inputs", bufs=1))
        weights = ctx.enter_context(tc.tile_pool(name="weights", bufs=1))
        stage = ctx.enter_context(tc.tile_pool(name="stage", bufs=2))
        stats = ctx.enter_context(tc.tile_pool(name="stats", bufs=3))
        quantised = ctx.enter_context(tc.tile_pool(name="quantised", bufs=4))
        results = ctx.enter_context(tc.tile_pool(name="results", bufs=3))
        turned = ctx.enter_context(tc.psum_pool(name="turned", bufs=4))
        sums = ctx.enter_context(tc.psum_pool(name="sums", bufs=1))
        products = ctx.enter_context(tc.psum_pool(name="products", bufs=3))

        identity = consts.tile([P, P], F32, name="identity")
        make_identity(nc, identity[:])
        minus_inv_batch = consts.tile([P, 1], BF16, name="minus_inv_batch")
        nc.vector.memset(minus_inv_batch[:], -1.0 / P)
        eps = consts.tile([P, 1], F32, name="eps")
        nc.vector.memset(eps[:], EPS)
        warm = consts.tile([P, 1], F32, name="warm")
        nc.scalar.activation(out=warm[:], in_=eps[:], func=ACT.Sqrt)

        vector_rows = consts.tile([P, P], F32, name="vector_rows")
        nc.vector.memset(vector_rows[:], 0.0)
        for v, vector in enumerate((s_g2, s_be2, c_g2, c_be2)):
            nc.sync.dma_start(
                out=vector_rows[:].bitcast(BF16)[QUARTERS * v : QUARTERS * (v + 1), :],
                in_=vector.rearrange("(q w) -> q w", q=QUARTERS),
            )

        def load_slices(chunk):
            rows = inputs.tile([P, CHUNK, FEATURES], BF16, name="s_rows%d" % chunk)
            nc.sync.dma_start(out=rows[:], in_=s_z2[:, chunk * CHUNK : (chunk + 1) * CHUNK, :])
            return rows

        def load_weight(w, label):
            halves = []
            for half in range(HALVES):
                rows = inputs.tile([P, N_TILE // P, FEATURES], BF16, name="%s%d" % (label, half))
                nc.sync.dma_start(
                    out=rows[:],
                    in_=w[half * N_TILE : (half + 1) * N_TILE, :].rearrange("(c p) k -> p c k", p=P),
                )
                halves.append(rows)
            return halves

        def load_bias(b, label):
            rows = consts.tile([P, OUTPUTS], BF16, name=label)
            nc.sync.dma_start(out=rows[:], in_=b.partition_broadcast(P))
            return rows

        c_rows = inputs.tile([P, FEATURES], BF16, name="c_rows")
        nc.sync.dma_start(out=c_rows[:], in_=c_z2)
        s_rows = [load_slices(0)]
        c_w_rows = load_weight(c_w3, "c_w_rows")
        c_bias_rows = load_bias(c_b3, "c_bias_rows")
        s_w_rows = load_weight(s_w3, "s_w_rows")
        s_bias_rows = load_bias(s_b3, "s_bias_rows")
        for chunk in range(1, SLICES // CHUNK):
            s_rows.append(load_slices(chunk))

        tables_ps = turned.tile([P, QUARTERS, P], F32, tag="turned", name="tables_ps")
        nc.tensor.transpose(tables_ps[:, 0, :], vector_rows[:], identity[:])
        tables = consts.tile([P, 4, PER_PARTITION], F32, name="tables")
        nc.vector.tensor_copy(
            out=tables[:].rearrange("p v j -> p (v j)"),
            in_=tables_ps[:, 0, 0 : 4 * QUARTERS].bitcast(BF16),
        )
        s_gain, s_shift = tables[:, 0, :], tables[:, 1, :]
        c_gain, c_shift = tables[:, 2, :], tables[:, 3, :]

        def halves_of(xt):
            return xt[:].bitcast(BF16).rearrange("p q (b e) -> p q e b", e=2)

        def blocks_of(group):
            if group == CONTEXT:
                return [c_rows[:]]
            first = group * PAIR
            return [s_rows[(first + s) // CHUNK][:, (first + s) % CHUNK, :] for s in range(PAIR)]

        def size_of(group):
            return len(blocks_of(group)) if CONTEXT <= group < PAIRS else 0

        xts, mean_ps, neg_mean, std = {}, {}, {}, {}
        scale, bias, hidden, grouped, codes, planes = {}, {}, {}, {}, {}, {}

        def turn(group, s):
            rows = blocks_of(group)[s]
            if s == 0:
                xts[group] = []
                mean_ps[group] = sums.tile(
                    [P, size_of(group), PER_PARTITION], F32, tag="mean_ps", name="mean_ps"
                )
            words = rows.bitcast(F32)
            xt = turned.tile([P, QUARTERS, P], F32, tag="turned", name="xt")
            for q in range(QUARTERS):
                nc.tensor.transpose(xt[:, q, :], words[:, q * P : (q + 1) * P], identity[:])
            xts[group].append(xt)
            by_parity = rows.rearrange("b (q p e) -> b q e p", q=QUARTERS, e=2)
            for q in range(QUARTERS):
                for e in range(2):
                    j = 2 * q + e
                    nc.tensor.matmul(
                        mean_ps[group][:, s, j : j + 1],
                        lhsT=by_parity[:, q, e, :],
                        rhs=minus_inv_batch[:],
                        start=True,
                        stop=True,
                    )

        def spread(group):
            shape = [P, size_of(group), PER_PARTITION]
            neg_mean[group] = stats.tile(shape, F32, tag="neg_mean", name="neg_mean")
            sq_sum = stats.tile(shape, F32, tag="sq_sum", name="sq_sum")
            for s, xt in enumerate(xts[group]):
                nc.scalar.copy(out=neg_mean[group][:, s, :], in_=mean_ps[group][:, s, :])
                squares = stage.tile([P, PER_PARTITION, P], BF16, tag="squares", name="squares")
                for q in range(QUARTERS):
                    for e in range(2):
                        j = 2 * q + e
                        nc.scalar.activation(
                            out=squares[:, j, :],
                            in_=halves_of(xt)[:, q, e, :],
                            func=ACT.Square,
                            bias=neg_mean[group][:, s, j : j + 1],
                            scale=1.0,
                            accum_out=sq_sum[:, s, j : j + 1],
                        )
            std[group] = stats.tile(shape, F32, tag="std", name="std")
            nc.scalar.activation(
                out=std[group][:], in_=sq_sum[:], func=ACT.Sqrt, bias=eps[:], scale=1.0 / P
            )

        def coefficient_steps(group):
            shape = [P, size_of(group), PER_PARTITION]
            gain, shift = (c_gain, c_shift) if group == CONTEXT else (s_gain, s_shift)
            inv_std = stats.tile(shape, F32, tag="inv_std", name="inv_std")
            centre = stats.tile(shape, F32, tag="centre", name="centre")
            scale[group] = stats.tile(shape, F32, tag="scale", name="scale")
            bias[group] = stats.tile(shape, F32, tag="bias", name="bias")
            return [
                lambda: nc.vector.reciprocal(out=inv_std[:], in_=std[group][:]),
                lambda: nc.vector.tensor_tensor(
                    out=scale[group][:],
                    in0=inv_std[:],
                    in1=gain.unsqueeze(1).to_broadcast(shape),
                    op=ALU.mult,
                ),
                lambda: nc.vector.tensor_tensor(
                    out=centre[:], in0=neg_mean[group][:], in1=scale[group][:], op=ALU.mult
                ),
                lambda: nc.vector.tensor_tensor(
                    out=bias[group][:],
                    in0=centre[:],
                    in1=shift.unsqueeze(1).to_broadcast(shape),
                    op=ALU.add,
                ),
            ]

        def activate(group, s):
            if s == 0:
                width = size_of(group) * PASSES * P
                hidden[group] = stage.tile([P, PACK, width], BF16, tag="hidden", name="hidden")
            for q in range(QUARTERS):
                for e in range(2):
                    j = 2 * q + e
                    g, t = j // PACK, j % PACK
                    first = (s * PASSES + g) * P
                    nc.scalar.activation(
                        out=hidden[group][:, t, first : first + P],
                        in_=halves_of(xts[group][s])[:, q, e, :],
                        func=ACT.Relu,
                        bias=bias[group][:, s, j : j + 1],
                        scale=scale[group][:, s, j : j + 1],
                    )

        def regroup_second_half(group):
            width = size_of(group) * PASSES * P
            middle = width // 2
            grouped[group] = stage.tile(
                [P, width, PACK], BF16, tag="grouped", name="grouped", align_bytes=64
            )
            nc.scalar.copy(
                out=grouped[group][:, middle:, :].rearrange("p (c i) t -> p c t i", i=4),
                in_=hidden[group][:, :, middle:].rearrange("p t (c i) -> p c t i", i=4),
            )

        def regroup_first_half(group):
            middle = size_of(group) * PASSES * P // 2
            nc.vector.tensor_copy(
                out=grouped[group][:, :middle, :].rearrange("p (c i) t -> p c t i", i=4),
                in_=hidden[group][:, :, :middle].rearrange("p t (c i) -> p c t i", i=4),
            )

        def quantise(group):
            width = size_of(group) * PASSES * P
            codes[group] = quantised.tile([P, width], U32, tag="codes", name="codes", align_bytes=64)
            planes[group] = quantised.tile([P, width], U8, tag="planes", name="planes", align_bytes=64)
            nc.vector.quantize_mx(
                out=codes[group][:].bitcast(FP8X4),
                scales=planes[group][:],
                in_=grouped[group][:].rearrange("p w t -> p (w t)"),
            )

        def weight_tiles(label):
            w_codes = weights.tile([P, PASSES, OUTPUTS], U32, name=label + "_codes", align_bytes=64)
            w_planes = weights.tile([P, PASSES, OUTPUTS], U8, name=label + "_planes", align_bytes=64)
            return w_codes, w_planes

        def quantise_weight_half(w_rows, w_codes, w_planes, half):
            words = w_rows[half][:].bitcast(F32)
            cols = slice(half * N_TILE, (half + 1) * N_TILE)
            for g in range(PASSES):
                grouped = stage.tile(
                    [P, N_TILE, PACK], BF16, tag="w_grouped", name="w_grouped", align_bytes=64
                )
                grouped_words = grouped[:].bitcast(F32)
                for bank in range(2):
                    wt = products.tile([P, 2, 2 * P], F32, tag="acc", name="wt")
                    for u in range(2):
                        q = 2 * g + u
                        for c in range(2):
                            nc.tensor.transpose(
                                wt[:, u, c * P : (c + 1) * P],
                                words[:, 2 * bank + c, q * P : (q + 1) * P],
                                identity[:],
                            )
                    target = grouped_words[:, bank * 2 * P : (bank + 1) * 2 * P, :]
                    if bank == 0:
                        nc.vector.tensor_copy(out=target, in_=wt[:].rearrange("p u n -> p n u"))
                    else:
                        nc.scalar.copy(out=target, in_=wt[:].rearrange("p u n -> p n u"))
                nc.vector.quantize_mx(
                    out=w_codes[:, g, cols].bitcast(FP8X4),
                    scales=w_planes[:, g, cols],
                    in_=grouped[:].rearrange("p n t -> p (n t)"),
                )

        def project(group, s, w_codes, w_planes, half):
            acc = products.tile([P, N_TILE], F32, tag="acc", name="acc")
            cols = slice(half * N_TILE, (half + 1) * N_TILE)
            for g in range(PASSES):
                rows = slice((s * PASSES + g) * P, (s * PASSES + g + 1) * P)
                nc.tensor.matmul_mx(
                    out=acc[:],
                    lhsT=codes[group][:, rows].bitcast(FP8X4),
                    lhsT_scale=planes[group][:, rows],
                    rhs=w_codes[:, g, cols].bitcast(FP8X4),
                    rhs_scale=w_planes[:, g, cols],
                    start=(g == 0),
                    stop=(g == PASSES - 1),
                )
            return acc

        c_w_codes, c_w_planes = weight_tiles("c_w")
        s_w_codes, s_w_planes = weight_tiles("s_w")

        gate = consts.tile([P, OUTPUTS], F32, name="gate")
        gated_bias = consts.tile([P, OUTPUTS], F32, name="gated_bias")
        best = consts.tile([P, PAIR, OUTPUTS], F32, name="best")
        gated = {}

        def open_gate():
            for half in range(HALVES):
                cols = slice(half * N_TILE, (half + 1) * N_TILE)
                acc = project(CONTEXT, 0, c_w_codes, c_w_planes, half)
                nc.vector.tensor_tensor(
                    out=gate[:, cols], in0=acc[:], in1=c_bias_rows[:, cols], op=ALU.add
                )
                nc.vector.tensor_tensor(
                    out=gated_bias[:, cols], in0=gate[:, cols], in1=s_bias_rows[:, cols], op=ALU.mult
                )

        def multiply(pair):
            if pair == 0:
                gated[pair] = best
            else:
                gated[pair] = results.tile([P, PAIR, OUTPUTS], F32, tag="gated", name="gated")
            for s in range(PAIR):
                for half in range(HALVES):
                    cols = slice(half * N_TILE, (half + 1) * N_TILE)
                    acc = project(pair, s, s_w_codes, s_w_planes, half)
                    nc.vector.tensor_tensor(
                        out=gated[pair][:, s, cols], in0=acc[:], in1=gate[:, cols], op=ALU.mult
                    )

        def add_bias_and_store(pair, s):
            biased = results.tile([P, OUTPUTS], F32, tag="biased", name="biased")
            nc.vector.tensor_tensor(
                out=biased[:], in0=gated[pair][:, s, :], in1=gated_bias[:], op=ALU.add
            )
            nc.sync.dma_start(out=out_0[:, pair * PAIR + s, :], in_=biased[:])

        def pool(pair, s):
            if pair > 0:
                nc.vector.tensor_tensor(
                    out=best[:, s, :], in0=best[:, s, :], in1=gated[pair][:, s, :], op=ALU.max
                )

        def step(n):
            if n == CONTEXT:
                open_gate()
            if n >= 0:
                multiply(n)
            if size_of(n + 2):
                spread(n + 2)
            for s in range(PAIR):
                if s < size_of(n + 1):
                    activate(n + 1, s)
                if s < size_of(n + 3):
                    turn(n + 3, s)
            if size_of(n + 1):
                regroup_second_half(n + 1)
            long_steps = []
            if n >= 0:
                long_steps.append(lambda: add_bias_and_store(n, 0))
            if size_of(n + 1):
                long_steps.append(lambda: regroup_first_half(n + 1))
            if n >= 0:
                long_steps.append(lambda: add_bias_and_store(n, 1))
            if size_of(n + 1):
                long_steps.append(lambda: quantise(n + 1))
            if n >= 0:
                long_steps.append(lambda: pool(n, 0))
                long_steps.append(lambda: pool(n, 1))
            short_steps = coefficient_steps(n + 2) if size_of(n + 2) else []
            for k in range(max(len(long_steps), len(short_steps))):
                if k < len(long_steps):
                    long_steps[k]()
                if k < len(short_steps):
                    short_steps[k]()

        step(CONTEXT - 3)
        step(CONTEXT - 2)
        for half in range(HALVES):
            quantise_weight_half(c_w_rows, c_w_codes, c_w_planes, half)
        step(CONTEXT - 1)
        for half in range(HALVES):
            quantise_weight_half(s_w_rows, s_w_codes, s_w_planes, half)
        step(CONTEXT)
        with tc.manual_schedule():
            for n in range(PAIRS):
                step(n)

        pooled = results.tile([P, OUTPUTS], F32, tag="biased", name="pooled")
        nc.vector.tensor_tensor(out=pooled[:], in0=best[:, 0, :], in1=best[:, 1, :], op=ALU.max)
        nc.vector.tensor_tensor(out=pooled[:], in0=pooled[:], in1=gated_bias[:], op=ALU.add)
        nc.sync.dma_start(out=out_1, in_=pooled[:])
